import numpy as np
import ml_dtypes


def mxq(x, axis, fmt="e4m3"):
    dtype, down = {"e4m3": (ml_dtypes.float8_e4m3fn, 7), "e5m2": (ml_dtypes.float8_e5m2, 14)}[fmt]
    v = np.moveaxis(np.asarray(x, np.float32).astype(ml_dtypes.bfloat16).astype(np.float64), axis, -1)
    blocks = v.reshape(v.shape[:-1] + (-1, 32))
    amax = np.abs(blocks).max(-1, keepdims=True)
    byte = np.maximum(np.where(amax > 0, np.frexp(amax)[1] - 1 + 127, 0) - down, 1)
    scale = np.exp2(byte - 127.0)
    codes = (blocks / scale).astype(np.float32).astype(dtype).astype(np.float64)
    return np.moveaxis((codes * scale).reshape(v.shape), -1, axis)


WIDE = False


def mx_kscale(k):
    if not WIDE:
        return np.ones(k)
    levels = np.array([10, -10, 5, -5, 0])
    a = np.random.permutation(np.resize(levels, k // 512 * 4)).reshape(k // 512, 4)
    idx = np.arange(k)
    return np.exp2(a[idx // 512, idx % 128 // 32])


BF16 = ml_dtypes.bfloat16


def bf(x):
    return np.asarray(x, np.float32).astype(BF16)


def f64(x):
    return np.asarray(x).astype(np.float64)


B, D, L0, L1, L2 = 4096, 512, 32, 512, 1024
KC = L1 + D
LN_EPS = 1e-5


def log_softmax(v):
    sh = v - v.max(-1, keepdims=True)
    return sh - np.log(np.exp(sh).sum(-1, keepdims=True))


def setup_inputs():
    s = mx_kscale(D)
    w = np.random.standard_normal((L2, KC)) * 1.5 / np.sqrt(KC)
    w[:, L1:] /= s
    return {"mid_logits": bf(np.random.standard_normal((B, L1)) * 3.0), "x": bf(np.random.standard_normal((B, D)) * s),
            "W2": bf(w), "b2": bf(np.random.standard_normal(L2) * 0.5)}


def reference(mid_logits, x, W2, b2):
    h = np.maximum(f64(mid_logits), 0.0)
    mu = h.mean(-1, keepdims=True)
    var = h.var(-1, keepdims=True)
    hn = (h - mu) / np.sqrt(var + LN_EPS)
    c = np.concatenate([hn, f64(x)], axis=1)
    li = (mxq(c, 1, "e4m3") @ mxq(f64(W2), 1, "e4m3").T) + f64(b2)
    return log_softmax(li)

@@ -1,0 +1,476 @@
+import math
+from contextlib import ExitStack
+
+import concourse.mybir as mybir
+from concourse.masks import make_identity
+
+F32 = mybir.dt.float32
+BF16 = mybir.dt.bfloat16
+U32 = mybir.dt.uint32
+U8 = mybir.dt.uint8
+I32 = mybir.dt.int32
+FP8X4 = mybir.dt.float8_e4m3fn_x4
+ALU = mybir.AluOpType
+ACT = mybir.ActivationFunctionType
+AX = mybir.AxisListType
+
+P = 128
+B, D, L1, L2 = 4096, 512, 512, 1024
+NT = B // P
+NPR = NT // 2
+GT = 4
+NG = NT // GT
+LN_EPS = 1e-5
+FLOPS = 2 * B * (L1 + D) * L2
+
+LN2 = math.log(2.0)
+ALPHA = LN2 / float(2 ** 23)
+BETA = LN2 * (0.043 - 127.0)
+
+PIN = False
+NIT = 4
+BATCHES = [[4 * g, 4 * g + 1, 4 * g + 2, 4 * g + 3] for g in range(7)] + [[28, 29], [30], [31]]
+EVH_ON_V = ()
+EVX_ON_S = tuple(range(16))
+RELU_ON_S = ()
+FIN_ENG = {30: "V", 31: "V"}
+
+
+def tile_bhcn_awx_pa_t_kernel(tc, mid_logits, x, W2, b2, out):
+    nc = tc.nc
+    m_v = mid_logits.rearrange("(p j) k -> p j k", j=NT)
+    x_v = x.rearrange("(p j) k -> p j k", j=NT)
+    o_v = out.rearrange("(p j) n -> p j n", j=NT)
+    w_v = W2.rearrange("(a p) k -> p a k", p=P)
+
+    with ExitStack() as ctx:
+        if PIN:
+            ctx.enter_context(tc.manual_schedule())
+        keep = ctx.enter_context(tc.tile_pool(name="keep", bufs=1))
+        work = ctx.enter_context(tc.tile_pool(name="work", bufs=4))
+        small = ctx.enter_context(tc.tile_pool(name="small", bufs=5))
+        lip = ctx.enter_context(tc.tile_pool(name="lip", bufs=7))
+        psum = ctx.enter_context(tc.psum_pool(name="psum", bufs=2))
+
+        m_ch = []
+        x_ch = []
+        w_ch = []
+        for g in range(NG):
+            m_ch.append(keep.tile([P, GT, L1], BF16, name="m%d" % g))
+            x_ch.append(keep.tile([P, GT, D], BF16, name="x%d" % g))
+        for c in range(4):
+            w_ch.append(keep.tile([P, 2, L1 + D], BF16, name="w%d" % c))
+        b_bc = keep.tile([P, L2], BF16, name="b_bc")
+
+        nc.sync.dma_start(out=m_ch[0][:], in_=m_v[:, 0:GT, :])
+        for c in range(4):
+            nc.sync.dma_start(out=w_ch[c][:], in_=w_v[:, 2 * c : 2 * c + 2, :])
+        nc.sync.dma_start(out=x_ch[0][:], in_=x_v[:, 0:GT, :])
+        nc.sync.dma_start(out=m_ch[1][:], in_=m_v[:, GT : 2 * GT, :])
+        nc.sync.dma_start(out=b_bc[:], in_=b2.partition_broadcast(P))
+        nc.sync.dma_start(out=x_ch[1][:], in_=x_v[:, GT : 2 * GT, :])
+        for g in range(2, NG):
+            nc.sync.dma_start(out=m_ch[g][:], in_=m_v[:, GT * g : GT * (g + 1), :])
+            nc.sync.dma_start(out=x_ch[g][:], in_=x_v[:, GT * g : GT * (g + 1), :])
+
+        ident_f = keep.tile([P, P], F32, name="ident_f")
+        ident_b = keep.tile([P, P], BF16, name="ident_b")
+        make_identity(nc, ident_f[:])
+        make_identity(nc, ident_b[:])
+        mhalf = keep.tile([P, GT], F32, name="mhalf")
+        nc.gpsimd.memset(mhalf[:], -0.5)
+
+        wgrp = keep.tile([P, 2, L2, 4], BF16, name="wgrp", align_bytes=64)
+        wc = keep.tile([P, 2, L2], U32, name="wc", align_bytes=64)
+        ws = keep.tile([P, 2, L2], U8, name="ws", align_bytes=64)
+
+        st = {}
+
+        def relu(pr):
+            g, c0 = pr // 2, 2 * (pr % 2)
+            if c0 == 0:
+                for nm in ("sum_h", "negmu", "ssq", "var", "rstd"):
+                    st[nm, g] = small.tile([P, GT], F32, name=nm)
+            h = work.tile([P, 2, L1], BF16, name="h", bufs=6)
+            for jj in range(2):
+                j = 2 * pr + jj
+                acc = st["sum_h", g][:, c0 + jj : c0 + jj + 1]
+                if pr in RELU_ON_S:
+                    nc.scalar.activation(
+                        out=h[:, jj, :], in_=m_ch[j // GT][:, j % GT, :], func=ACT.Relu, accum_out=acc
+                    )
+                else:
+                    nc.vector.tensor_scalar(
+                        out=h[:, jj, :],
+                        in0=m_ch[j // GT][:, j % GT, :],
+                        scalar1=0.0,
+                        scalar2=None,
+                        op0=ALU.max,
+                        op1=ALU.add,
+                        accum_out=acc,
+                    )
+            st["h", pr] = h
+
+        def s_sq(pr):
+            g, c0 = pr // 2, 2 * (pr % 2)
+            h = st["h", pr]
+            nc.scalar.mul(out=st["negmu", g][:, c0 : c0 + 2], in_=st["sum_h", g][:, c0 : c0 + 2], mul=-1.0 / L1)
+            for jj in range(2):
+                sqj = work.tile([P, L1], BF16, name="sqj", bufs=2)
+                nc.scalar.activation(
+                    out=sqj[:],
+                    in_=h[:, jj, :],
+                    func=ACT.Square,
+                    bias=st["negmu", g][:, c0 + jj : c0 + jj + 1],
+                    accum_out=st["ssq", g][:, c0 + jj : c0 + jj + 1],
+                )
+
+        def g_sm(g, c0, n):
+            cs = slice(c0, c0 + n)
+            var, rstd = (st[nm, g][:, cs] for nm in ("var", "rstd"))
+            nc.gpsimd.tensor_scalar(
+                out=var, in0=st["ssq", g][:, cs], scalar1=1.0 / L1, scalar2=LN_EPS, op0=ALU.mult, op1=ALU.add
+            )
+            nc.gpsimd.tensor_tensor(out=rstd, in0=var, in1=mhalf[:, 0:n], op=ALU.pow)
+
+        def g_norm(pr):
+            g, c0 = pr // 2, 2 * (pr % 2)
+            h = st["h", pr]
+            hnp = work.tile([P, 2, 4, P], BF16, name="hnp")
+            for jj in range(2):
+                nc.gpsimd.tensor_scalar(
+                    out=hnp[:, jj, :, :].rearrange("p (u e) q -> p u e q", u=2),
+                    in0=h[:, jj, :].rearrange("p (u q e) -> p u e q", u=2, e=2),
+                    scalar1=st["negmu", g][:, c0 + jj : c0 + jj + 1],
+                    scalar2=st["rstd", g][:, c0 + jj : c0 + jj + 1],
+                    op0=ALU.add,
+                    op1=ALU.mult,
+                )
+            st["hnp", pr] = hnp
+
+        def pe_th(pr):
+            hnp = st["hnp", pr]
+            th = psum.tile([P, 2, 4, P], BF16, name="th")
+            for jj in range(2):
+                for t in range(4):
+                    nc.tensor.transpose(out=th[:, jj, t, :], in_=hnp[:, jj, t, :], identity=ident_b[:])
+            st["th", pr] = th
+
+        def evh(pr):
+            th = st["th", pr]
+            hg = work.tile([P, 2, P, 4], BF16, name="hg", align_bytes=64)
+            src = th[:].rearrange("q j t b -> q j b t")
+            if pr in EVH_ON_V:
+                nc.vector.tensor_copy(out=hg[:], in_=src)
+            else:
+                nc.scalar.copy(out=hg[:], in_=src)
+            st["hg", pr] = hg
+
+        def v_qh(pr):
+            hg = st["hg", pr]
+            hc = work.tile([P, 2 * P], U32, name="hc", align_bytes=64)
+            hs = work.tile([P, 2 * P], U8, name="hs", align_bytes=64)
+            nc.vector.quantize_mx(
+                out=hc[:].bitcast(FP8X4), scales=hs[:], in_=hg[:].rearrange("p j b t -> p (j b t)")
+            )
+            st["hq", pr] = (hc, hs)
+
+        def pe_tx(pr):
+            tx = psum.tile([P, 2, 2, P], F32, name="tx")
+            for jj in range(2):
+                j = 2 * pr + jj
+                xw = x_ch[j // GT][:, j % GT, :].bitcast(F32)
+                for u in range(2):
+                    nc.tensor.transpose(
+                        out=tx[:, jj, u, :], in_=xw[:, P * u : P * (u + 1)], identity=ident_f[:]
+                    )
+            st["tx", pr] = tx
+
+        def evx(pr):
+            tx = st["tx", pr]
+            xg = work.tile([P, 2, P, 4], BF16, name="xg", align_bytes=64)
+            src = tx[:].rearrange("q j u b -> q j b u")
+            if pr in EVX_ON_S:
+                nc.scalar.copy(out=xg[:].bitcast(F32), in_=src)
+            else:
+                nc.vector.tensor_copy(out=xg[:].bitcast(F32), in_=src)
+            st["xg", pr] = xg
+
+        def v_qx(pr):
+            xg = st["xg", pr]
+            xc = work.tile([P, 2 * P], U32, name="xc", align_bytes=64, bufs=6)
+            xs = work.tile([P, 2 * P], U8, name="xs", align_bytes=64, bufs=6)
+            nc.vector.quantize_mx(
+                out=xc[:].bitcast(FP8X4), scales=xs[:], in_=xg[:].rearrange("p j b t -> p (j b t)")
+            )
+            st["xq", pr] = (xc, xs)
+
+        def w_t(a):
+            tw = psum.tile([P, 2, 2, P], F32, name="tw", tag="po", bufs=4)
+            ww = w_ch[a // 2][:, a % 2, :].bitcast(F32)
+            for g in range(2):
+                for u in range(2):
+                    c0 = 256 * g + P * u
+                    nc.tensor.transpose(out=tw[:, g, u, :], in_=ww[:, c0 : c0 + P], identity=ident_f[:])
+            st["tw", a] = tw
+
+        def w_ev(a, on_v):
+            src = st["tw", a][:].rearrange("q g u n -> q g n u")
+            dst = wgrp[:].bitcast(F32)[:, :, a * P : (a + 1) * P, :]
+            if on_v:
+                nc.vector.tensor_copy(out=dst, in_=src)
+            else:
+                nc.scalar.copy(out=dst, in_=src)
+
+        def w_q(hf):
+            cols = slice(hf * 512, (hf + 1) * 512)
+            for g in range(2):
+                nc.vector.quantize_mx(
+                    out=wc[:, g, cols].bitcast(FP8X4),
+                    scales=ws[:, g, cols],
+                    in_=wgrp[:, g, cols, :].rearrange("p n t -> p (n t)"),
+                )
+
+        def pe_mm(j):
+            pr, jj = j // 2, j % 2
+            bcols = slice(jj * P, (jj + 1) * P)
+            pos = []
+            for hf in range(2):
+                pos.append(psum.tile([P, 512], F32, name="po", tag="po", bufs=4))
+            for g, (cc, ss) in enumerate((st["hq", pr], st["xq", pr])):
+                for hf in range(2):
+                    cols = slice(hf * 512, (hf + 1) * 512)
+                    nc.tensor.matmul_mx(
+                        out=pos[hf][:],
+                        lhsT=cc[:, bcols].bitcast(FP8X4),
+                        lhsT_scale=ss[:, bcols],
+                        rhs=wc[:, g, cols].bitcast(FP8X4),
+                        rhs_scale=ws[:, g, cols],
+                        start=(g == 0),
+                        stop=(g == 1),
+                    )
+            st["po", j] = pos
+
+        def v_a(j):
+            if j % 2 == 0:
+                st["li", j // 2] = lip.tile([P, 2, L2], F32, name="li")
+            li = st["li", j // 2]
+            pos = st["po", j]
+            for hf in range(2):
+                cols = slice(hf * 512, (hf + 1) * 512)
+                nc.vector.tensor_tensor(out=li[:, j % 2, cols], in0=pos[hf][:], in1=b_bc[:, cols], op=ALU.add)
+
+        def bt_of(j):
+            for bi, bt in enumerate(BATCHES):
+                if j in bt:
+                    return bi, bt.index(j)
+            return None
+
+        def v_max(j):
+            bi, c = bt_of(j)
+            if c == 0:
+                st["negM", bi] = small.tile([P, GT], F32, name="negM")
+                st["sume", bi] = small.tile([P, GT], F32, name="sume")
+            li = st["li", j // 2]
+            mx = work.tile([P, 512], BF16, name="mx", bufs=2)
+            mj = work.tile([P, 512], BF16, name="mj", bufs=2)
+            nc.vector.tensor_tensor(out=mx[:], in0=li[:, j % 2, 0:512], in1=li[:, j % 2, 512:1024], op=ALU.max)
+            nc.vector.tensor_scalar(
+                out=mj[:],
+                in0=mx[:],
+                scalar1=-1.0,
+                scalar2=None,
+                op0=ALU.mult,
+                op1=ALU.min,
+                accum_out=st["negM", bi][:, c : c + 1],
+            )
+
+        def s_exp(j):
+            bi, c = bt_of(j)
+            li = st["li", j // 2]
+            ej = work.tile([P, L2], BF16, name="ej", bufs=2)
+            nc.scalar.activation(
+                out=ej[:],
+                in_=li[:, j % 2, :],
+                func=ACT.Exp,
+                bias=st["negM", bi][:, c : c + 1],
+                accum_out=st["sume", bi][:, c : c + 1],
+            )
+
+        def v_n0(bi):
+            n = len(BATCHES[bi])
+            sc = small.tile([P, GT], F32, name="sc")
+            y = small.tile([P, GT], F32, name="y0")
+            nc.vector.tensor_copy(out=sc[:, 0:n], in_=st["sume", bi][:, 0:n])
+            nc.vector.tensor_scalar(
+                out=y[:, 0:n], in0=sc[:, 0:n].bitcast(I32), scalar1=ALPHA, scalar2=BETA, op0=ALU.mult, op1=ALU.add
+            )
+            st["y", bi] = y
+
+        def s_ne(bi):
+            n = len(BATCHES[bi])
+            e = small.tile([P, GT], F32, name="e")
+            nc.scalar.activation(out=e[:, 0:n], in_=st["y", bi][:, 0:n], func=ACT.Exp, scale=-1.0)
+            st["e", bi] = e
+
+        def v_nu(bi, last):
+            n = len(BATCHES[bi])
+            u = small.tile([P, GT], F32, name="u")
+            y2 = small.tile([P, GT], F32, name="y2")
+            nc.vector.tensor_tensor(out=u[:, 0:n], in0=st["e", bi][:, 0:n], in1=st["sume", bi][:, 0:n], op=ALU.mult)
+            nc.vector.scalar_tensor_tensor(
+                out=y2[:, 0:n], in0=u[:, 0:n], scalar=-1.0, in1=st["y", bi][:, 0:n], op0=ALU.add, op1=ALU.add
+            )
+            st["y", bi] = y2
+            if last:
+                nsh = small.tile([P, GT], F32, name="nsh")
+                nc.vector.tensor_tensor(out=nsh[:, 0:n], in0=st["negM", bi][:, 0:n], in1=y2[:, 0:n], op=ALU.subtract)
+                st["nsh", bi] = nsh
+
+        def fin(j, eng):
+            bi, c = bt_of(j)
+            li = st["li", j // 2]
+            nsh = st["nsh", bi]
+            if eng == "G":
+                nc.gpsimd.tensor_scalar(
+                    out=li[:, j % 2, :],
+                    in0=li[:, j % 2, :],
+                    scalar1=nsh[:, c : c + 1],
+                    scalar2=1.0,
+                    op0=ALU.add,
+                    op1=ALU.mult,
+                )
+            else:
+                nc.vector.tensor_scalar(
+                    out=li[:, j % 2, :], in0=li[:, j % 2, :], scalar1=nsh[:, c : c + 1], scalar2=None, op0=ALU.add
+                )
+
+        def store(j0, n):
+            li = st["li", j0 // 2]
+            nc.sync.dma_start(out=o_v[:, j0 : j0 + n, :], in_=li[:, j0 % 2 : j0 % 2 + n, :])
+
+        def ok(pr):
+            return 0 <= pr < NPR
+
+        pending = []
+        fin_q = []
+
+        def newton_v():
+            for item in pending:
+                if item[1] % 2 == 0 and item[1] <= 2 * NIT:
+                    if item[1] == 0:
+                        v_n0(item[0])
+                    else:
+                        v_nu(item[0], item[1] == 2 * NIT)
+                    item[1] += 1
+                    break
+            while pending and pending[0][1] == 2 * NIT + 1:
+                fin_q.extend(BATCHES[pending.pop(0)[0]])
+
+        def newton_s():
+            for item in pending:
+                if item[1] % 2 == 1:
+                    s_ne(item[0])
+                    item[1] += 1
+                    break
+
+        def exp_start(j):
+            s_exp(j)
+            for bi, bt in enumerate(BATCHES):
+                if bt[-1] == j:
+                    pending.append([bi, 0])
+
+        def g_fin(k):
+            for i in range(k):
+                if fin_q:
+                    j = fin_q.pop(0)
+                    fin(j, FIN_ENG.get(j, "G"))
+                    if j >= NT - 2:
+                        store(j, 1)
+                    elif j % 2 == 1:
+                        store(j - 1, 2)
+
+        relu(0)
+        s_sq(0)
+        g_sm(0, 0, 2)
+        g_norm(0)
+        relu(1)
+        s_sq(1)
+        g_sm(0, 2, 2)
+        g_norm(1)
+        for a in range(8):
+            w_t(a)
+            w_ev(a, a % 2 == 0)
+            if a % 4 == 3:
+                w_q(a // 4)
+        pe_th(0)
+        pe_tx(0)
+        evh(0)
+        v_qh(0)
+        evx(0)
+        v_qx(0)
+        pe_mm(0)
+        pe_mm(1)
+        pe_th(1)
+        pe_tx(1)
+        for pr in (2, 3):
+            relu(pr)
+            s_sq(pr)
+        evh(1)
+        evx(1)
+        g_sm(1, 0, GT)
+        g_norm(2)
+        pe_tx(2)
+        evx(2)
+        relu(4)
+        s_sq(4)
+        relu(5)
+
+        for s in range(NPR):
+            j0, j1 = 2 * s, 2 * s + 1
+            if s % 2 == 1 and ok(s + 3):
+                g_sm((s + 3) // 2, 0, GT)
+            if ok(s + 3):
+                g_norm(s + 3)
+            if s > 0:
+                exp_start(j0 - 1)
+            v_a(j0)
+            newton_v()
+            if ok(s + 5):
+                s_sq(s + 5)
+            newton_s()
+            v_max(j0)
+            if ok(s + 1):
+                v_qh(s + 1)
+                if s == 0:
+                    v_qx(1)
+            newton_v()
+            if ok(s + 1):
+                pe_mm(j0 + 2)
+            if ok(s + 2):
+                pe_th(s + 2)
+            if ok(s + 3):
+                pe_tx(s + 3)
+            exp_start(j0)
+            g_fin(1)
+            v_a(j1)
+            newton_v()
+            if ok(s + 1):
+                pe_mm(j1 + 2)
+            if ok(s + 3):
+                evx(s + 3)
+            newton_s()
+            v_max(j1)
+            if ok(s + 2):
+                evh(s + 2)
+                v_qx(s + 2)
+            newton_s()
+            if ok(s + 6):
+                relu(s + 6)
+            newton_v()
+            g_fin(1)
+        exp_start(NT - 1)
+        while pending or fin_q:
+            newton_v()
+            newton_s()
+            g_fin(4)

@@ -31,8 +31,8 @@ PIN = False
 NIT = 4
 BATCHES = [[4 * g, 4 * g + 1, 4 * g + 2, 4 * g + 3] for g in range(7)] + [[28, 29], [30], [31]]
 EVH_ON_V = ()
-EVX_ON_S = tuple(range(16))
-RELU_ON_S = ()
+EVX_ON_S = ()
+RELU_ON_S = tuple(range(16))
 FIN_ENG = {30: "V", 31: "V"}
 
 
@@ -158,22 +158,26 @@ def tile_bhcn_awx_pa_t_kernel(tc, mid_logits, x, W2, b2, out):
 
         def evh(pr):
             th = st["th", pr]
-            hg = work.tile([P, 2, P, 4], BF16, name="hg", align_bytes=64)
+            hg = grouped(pr)[:, 0, :, :, :]
             src = th[:].rearrange("q j t b -> q j b t")
             if pr in EVH_ON_V:
-                nc.vector.tensor_copy(out=hg[:], in_=src)
+                nc.vector.tensor_copy(out=hg, in_=src)
             else:
-                nc.scalar.copy(out=hg[:], in_=src)
-            st["hg", pr] = hg
+                nc.scalar.copy(out=hg, in_=src)
 
-        def v_qh(pr):
-            hg = st["hg", pr]
-            hc = work.tile([P, 2 * P], U32, name="hc", align_bytes=64)
-            hs = work.tile([P, 2 * P], U8, name="hs", align_bytes=64)
+        def grouped(pr):
+            if ("cg", pr) not in st:
+                st["cg", pr] = work.tile([P, 2, 2, P, 4], BF16, name="cg", align_bytes=64)
+            return st["cg", pr]
+
+        def v_q(pr):
+            cg = st["cg", pr]
+            cc = work.tile([P, 4 * P], U32, name="cc", align_bytes=64)
+            cs = work.tile([P, 4 * P], U8, name="cs", align_bytes=64)
             nc.vector.quantize_mx(
-                out=hc[:].bitcast(FP8X4), scales=hs[:], in_=hg[:].rearrange("p j b t -> p (j b t)")
+                out=cc[:].bitcast(FP8X4), scales=cs[:], in_=cg[:].rearrange("p g j b t -> p (g j b t)")
             )
-            st["hq", pr] = (hc, hs)
+            st["cq", pr] = (cc, cs)
 
         def pe_tx(pr):
             tx = psum.tile([P, 2, 2, P], F32, name="tx")
@@ -188,22 +192,12 @@ def tile_bhcn_awx_pa_t_kernel(tc, mid_logits, x, W2, b2, out):
 
         def evx(pr):
             tx = st["tx", pr]
-            xg = work.tile([P, 2, P, 4], BF16, name="xg", align_bytes=64)
+            xg = grouped(pr)[:, 1, :, :, :].bitcast(F32)
             src = tx[:].rearrange("q j u b -> q j b u")
             if pr in EVX_ON_S:
-                nc.scalar.copy(out=xg[:].bitcast(F32), in_=src)
+                nc.scalar.copy(out=xg, in_=src)
             else:
-                nc.vector.tensor_copy(out=xg[:].bitcast(F32), in_=src)
-            st["xg", pr] = xg
-
-        def v_qx(pr):
-            xg = st["xg", pr]
-            xc = work.tile([P, 2 * P], U32, name="xc", align_bytes=64, bufs=6)
-            xs = work.tile([P, 2 * P], U8, name="xs", align_bytes=64, bufs=6)
-            nc.vector.quantize_mx(
-                out=xc[:].bitcast(FP8X4), scales=xs[:], in_=xg[:].rearrange("p j b t -> p (j b t)")
-            )
-            st["xq", pr] = (xc, xs)
+                nc.vector.tensor_copy(out=xg, in_=src)
 
         def w_t(a):
             tw = psum.tile([P, 2, 2, P], F32, name="tw", tag="po", bufs=4)
@@ -233,11 +227,12 @@ def tile_bhcn_awx_pa_t_kernel(tc, mid_logits, x, W2, b2, out):
 
         def pe_mm(j):
             pr, jj = j // 2, j % 2
-            bcols = slice(jj * P, (jj + 1) * P)
+            cc, ss = st["cq", pr]
             pos = []
             for hf in range(2):
                 pos.append(psum.tile([P, 512], F32, name="po", tag="po", bufs=4))
-            for g, (cc, ss) in enumerate((st["hq", pr], st["xq", pr])):
+            for g in range(2):
+                bcols = slice((2 * g + jj) * P, (2 * g + jj + 1) * P)
                 for hf in range(2):
                     cols = slice(hf * 512, (hf + 1) * 512)
                     nc.tensor.matmul_mx(
@@ -272,17 +267,8 @@ def tile_bhcn_awx_pa_t_kernel(tc, mid_logits, x, W2, b2, out):
                 st["negM", bi] = small.tile([P, GT], F32, name="negM")
                 st["sume", bi] = small.tile([P, GT], F32, name="sume")
             li = st["li", j // 2]
-            mx = work.tile([P, 512], BF16, name="mx", bufs=2)
-            mj = work.tile([P, 512], BF16, name="mj", bufs=2)
-            nc.vector.tensor_tensor(out=mx[:], in0=li[:, j % 2, 0:512], in1=li[:, j % 2, 512:1024], op=ALU.max)
-            nc.vector.tensor_scalar(
-                out=mj[:],
-                in0=mx[:],
-                scalar1=-1.0,
-                scalar2=None,
-                op0=ALU.mult,
-                op1=ALU.min,
-                accum_out=st["negM", bi][:, c : c + 1],
+            nc.vector.tensor_reduce(
+                out=st["negM", bi][:, c : c + 1], in_=li[:, j % 2, :], axis=AX.X, op=ALU.max, negate=True
             )
 
         def s_exp(j):
@@ -406,9 +392,8 @@ def tile_bhcn_awx_pa_t_kernel(tc, mid_logits, x, W2, b2, out):
         pe_th(0)
         pe_tx(0)
         evh(0)
-        v_qh(0)
         evx(0)
-        v_qx(0)
+        v_q(0)
         pe_mm(0)
         pe_mm(1)
         pe_th(1)
@@ -441,9 +426,7 @@ def tile_bhcn_awx_pa_t_kernel(tc, mid_logits, x, W2, b2, out):
             newton_s()
             v_max(j0)
             if ok(s + 1):
-                v_qh(s + 1)
-                if s == 0:
-                    v_qx(1)
+                v_q(s + 1)
             newton_v()
             if ok(s + 1):
                 pe_mm(j0 + 2)
@@ -463,7 +446,6 @@ def tile_bhcn_awx_pa_t_kernel(tc, mid_logits, x, W2, b2, out):
             v_max(j1)
             if ok(s + 2):
                 evh(s + 2)
-                v_qx(s + 2)
             newton_s()
             if ok(s + 6):
                 relu(s + 6)

@@ -31,9 +31,9 @@ PIN = False
 NIT = 4
 BATCHES = [[4 * g, 4 * g + 1, 4 * g + 2, 4 * g + 3] for g in range(7)] + [[28, 29], [30], [31]]
 EVH_ON_V = ()
-EVX_ON_S = ()
-RELU_ON_S = tuple(range(16))
-FIN_ENG = {30: "V", 31: "V"}
+EVX_ON_S = tuple(range(16))
+RELU_ON_S = ()
+FIN_ENG = dict((j, "S" if j % 2 == 1 else "V") for j in range(32))
 
 
 def tile_bhcn_awx_pa_t_kernel(tc, mid_logits, x, W2, b2, out):
@@ -138,9 +138,9 @@ def tile_bhcn_awx_pa_t_kernel(tc, mid_logits, x, W2, b2, out):
             h = st["h", pr]
             hnp = work.tile([P, 2, 4, P], BF16, name="hnp")
             for jj in range(2):
-                nc.gpsimd.tensor_scalar(
-                    out=hnp[:, jj, :, :].rearrange("p (u e) q -> p u e q", u=2),
-                    in0=h[:, jj, :].rearrange("p (u q e) -> p u e q", u=2, e=2),
+                nc.vector.tensor_scalar(
+                    out=hnp[:, jj, :, :].rearrange("p t q -> p (t q)"),
+                    in0=h[:, jj, :],
                     scalar1=st["negmu", g][:, c0 + jj : c0 + jj + 1],
                     scalar2=st["rstd", g][:, c0 + jj : c0 + jj + 1],
                     op0=ALU.add,
@@ -199,22 +199,26 @@ def tile_bhcn_awx_pa_t_kernel(tc, mid_logits, x, W2, b2, out):
             else:
                 nc.vector.tensor_copy(out=xg, in_=src)
 
-        def w_t(a):
-            tw = psum.tile([P, 2, 2, P], F32, name="tw", tag="po", bufs=4)
-            ww = w_ch[a // 2][:, a % 2, :].bitcast(F32)
-            for g in range(2):
+        def w_t(ap):
+            twh = psum.tile([P, 2, 4, P], BF16, name="twh", tag="th")
+            twx = psum.tile([P, 2, 2, P], F32, name="twx", tag="tx")
+            for aa in range(2):
+                wrow = w_ch[ap][:, aa, :]
+                for t in range(4):
+                    nc.tensor.transpose(out=twh[:, aa, t, :], in_=wrow[:, P * t : P * (t + 1)], identity=ident_b[:])
+                ww = wrow.bitcast(F32)
                 for u in range(2):
-                    c0 = 256 * g + P * u
-                    nc.tensor.transpose(out=tw[:, g, u, :], in_=ww[:, c0 : c0 + P], identity=ident_f[:])
-            st["tw", a] = tw
-
-        def w_ev(a, on_v):
-            src = st["tw", a][:].rearrange("q g u n -> q g n u")
-            dst = wgrp[:].bitcast(F32)[:, :, a * P : (a + 1) * P, :]
-            if on_v:
-                nc.vector.tensor_copy(out=dst, in_=src)
-            else:
-                nc.scalar.copy(out=dst, in_=src)
+                    c0 = 256 + P * u
+                    nc.tensor.transpose(out=twx[:, aa, u, :], in_=ww[:, c0 : c0 + P], identity=ident_f[:])
+            rows = slice(2 * P * ap, 2 * P * (ap + 1))
+            nc.vector.tensor_copy(
+                out=wgrp[:, 0, rows, :].rearrange("p (a n) t -> p a n t", a=2),
+                in_=twh[:].rearrange("q a t n -> q a n t"),
+            )
+            nc.scalar.copy(
+                out=wgrp[:, 1, rows, :].bitcast(F32).rearrange("p (a n) u -> p a n u", a=2),
+                in_=twx[:].rearrange("q a u n -> q a n u"),
+            )
 
         def w_q(hf):
             cols = slice(hf * 512, (hf + 1) * 512)
@@ -267,8 +271,17 @@ def tile_bhcn_awx_pa_t_kernel(tc, mid_logits, x, W2, b2, out):
                 st["negM", bi] = small.tile([P, GT], F32, name="negM")
                 st["sume", bi] = small.tile([P, GT], F32, name="sume")
             li = st["li", j // 2]
-            nc.vector.tensor_reduce(
-                out=st["negM", bi][:, c : c + 1], in_=li[:, j % 2, :], axis=AX.X, op=ALU.max, negate=True
+            mx = work.tile([P, 512], BF16, name="mx", bufs=2)
+            mj = work.tile([P, 512], BF16, name="mj", bufs=2)
+            nc.vector.tensor_tensor(out=mx[:], in0=li[:, j % 2, 0:512], in1=li[:, j % 2, 512:1024], op=ALU.max)
+            nc.vector.tensor_scalar(
+                out=mj[:],
+                in0=mx[:],
+                scalar1=-1.0,
+                scalar2=None,
+                op0=ALU.mult,
+                op1=ALU.min,
+                accum_out=st["negM", bi][:, c : c + 1],
             )
 
         def s_exp(j):
@@ -325,6 +338,10 @@ def tile_bhcn_awx_pa_t_kernel(tc, mid_logits, x, W2, b2, out):
                     scalar2=1.0,
                     op0=ALU.add,
                     op1=ALU.mult,
+                )
+            elif eng == "S":
+                nc.scalar.activation(
+                    out=li[:, j % 2, :], in_=li[:, j % 2, :], func=ACT.Identity, bias=nsh[:, c : c + 1]
                 )
             else:
                 nc.vector.tensor_scalar(
@@ -384,11 +401,10 @@ def tile_bhcn_awx_pa_t_kernel(tc, mid_logits, x, W2, b2, out):
         s_sq(1)
         g_sm(0, 2, 2)
         g_norm(1)
-        for a in range(8):
-            w_t(a)
-            w_ev(a, a % 2 == 0)
-            if a % 4 == 3:
-                w_q(a // 4)
+        for ap in range(4):
+            w_t(ap)
+            if ap % 2 == 1:
+                w_q(ap // 2)
         pe_th(0)
         pe_tx(0)
         evh(0)

@@ -27,13 +27,13 @@ LN2 = math.log(2.0)
 ALPHA = LN2 / float(2 ** 23)
 BETA = LN2 * (0.043 - 127.0)
 
-PIN = False
+PIN = True
 NIT = 4
 BATCHES = [[4 * g, 4 * g + 1, 4 * g + 2, 4 * g + 3] for g in range(7)] + [[28, 29], [30], [31]]
-EVH_ON_V = ()
-EVX_ON_S = tuple(range(16))
-RELU_ON_S = ()
-FIN_ENG = dict((j, "S" if j % 2 == 1 else "V") for j in range(32))
+EVH_ON_V = (0, 1)
+EVX_ON_S = ()
+RELU_ON_S = tuple(range(16))
+FIN_ENG = {30: "V", 31: "V"}
 
 
 def tile_bhcn_awx_pa_t_kernel(tc, mid_logits, x, W2, b2, out):
@@ -138,9 +138,9 @@ def tile_bhcn_awx_pa_t_kernel(tc, mid_logits, x, W2, b2, out):
             h = st["h", pr]
             hnp = work.tile([P, 2, 4, P], BF16, name="hnp")
             for jj in range(2):
-                nc.vector.tensor_scalar(
-                    out=hnp[:, jj, :, :].rearrange("p t q -> p (t q)"),
-                    in0=h[:, jj, :],
+                nc.gpsimd.tensor_scalar(
+                    out=hnp[:, jj, :, :].rearrange("p (u e) q -> p u e q", u=2),
+                    in0=h[:, jj, :].rearrange("p (u q e) -> p u e q", u=2, e=2),
                     scalar1=st["negmu", g][:, c0 + jj : c0 + jj + 1],
                     scalar2=st["rstd", g][:, c0 + jj : c0 + jj + 1],
                     op0=ALU.add,
@@ -199,26 +199,22 @@ def tile_bhcn_awx_pa_t_kernel(tc, mid_logits, x, W2, b2, out):
             else:
                 nc.vector.tensor_copy(out=xg, in_=src)
 
-        def w_t(ap):
-            twh = psum.tile([P, 2, 4, P], BF16, name="twh", tag="th")
-            twx = psum.tile([P, 2, 2, P], F32, name="twx", tag="tx")
-            for aa in range(2):
-                wrow = w_ch[ap][:, aa, :]
-                for t in range(4):
-                    nc.tensor.transpose(out=twh[:, aa, t, :], in_=wrow[:, P * t : P * (t + 1)], identity=ident_b[:])
-                ww = wrow.bitcast(F32)
+        def w_t(a):
+            tw = psum.tile([P, 2, 2, P], F32, name="tw", tag="po", bufs=4)
+            ww = w_ch[a // 2][:, a % 2, :].bitcast(F32)
+            for g in range(2):
                 for u in range(2):
-                    c0 = 256 + P * u
-                    nc.tensor.transpose(out=twx[:, aa, u, :], in_=ww[:, c0 : c0 + P], identity=ident_f[:])
-            rows = slice(2 * P * ap, 2 * P * (ap + 1))
-            nc.vector.tensor_copy(
-                out=wgrp[:, 0, rows, :].rearrange("p (a n) t -> p a n t", a=2),
-                in_=twh[:].rearrange("q a t n -> q a n t"),
-            )
-            nc.scalar.copy(
-                out=wgrp[:, 1, rows, :].bitcast(F32).rearrange("p (a n) u -> p a n u", a=2),
-                in_=twx[:].rearrange("q a u n -> q a n u"),
-            )
+                    c0 = 256 * g + P * u
+                    nc.tensor.transpose(out=tw[:, g, u, :], in_=ww[:, c0 : c0 + P], identity=ident_f[:])
+            st["tw", a] = tw
+
+        def w_ev(a, on_v):
+            src = st["tw", a][:].rearrange("q g u n -> q g n u")
+            dst = wgrp[:].bitcast(F32)[:, :, a * P : (a + 1) * P, :]
+            if on_v:
+                nc.vector.tensor_copy(out=dst, in_=src)
+            else:
+                nc.scalar.copy(out=dst, in_=src)
 
         def w_q(hf):
             cols = slice(hf * 512, (hf + 1) * 512)
@@ -271,17 +267,8 @@ def tile_bhcn_awx_pa_t_kernel(tc, mid_logits, x, W2, b2, out):
                 st["negM", bi] = small.tile([P, GT], F32, name="negM")
                 st["sume", bi] = small.tile([P, GT], F32, name="sume")
             li = st["li", j // 2]
-            mx = work.tile([P, 512], BF16, name="mx", bufs=2)
-            mj = work.tile([P, 512], BF16, name="mj", bufs=2)
-            nc.vector.tensor_tensor(out=mx[:], in0=li[:, j % 2, 0:512], in1=li[:, j % 2, 512:1024], op=ALU.max)
-            nc.vector.tensor_scalar(
-                out=mj[:],
-                in0=mx[:],
-                scalar1=-1.0,
-                scalar2=None,
-                op0=ALU.mult,
-                op1=ALU.min,
-                accum_out=st["negM", bi][:, c : c + 1],
+            nc.vector.tensor_reduce(
+                out=st["negM", bi][:, c : c + 1], in_=li[:, j % 2, :], axis=AX.X, op=ALU.max, negate=True
             )
 
         def s_exp(j):
@@ -339,10 +326,6 @@ def tile_bhcn_awx_pa_t_kernel(tc, mid_logits, x, W2, b2, out):
                     op0=ALU.add,
                     op1=ALU.mult,
                 )
-            elif eng == "S":
-                nc.scalar.activation(
-                    out=li[:, j % 2, :], in_=li[:, j % 2, :], func=ACT.Identity, bias=nsh[:, c : c + 1]
-                )
             else:
                 nc.vector.tensor_scalar(
                     out=li[:, j % 2, :], in0=li[:, j % 2, :], scalar1=nsh[:, c : c + 1], scalar2=None, op0=ALU.add
@@ -397,14 +380,18 @@ def tile_bhcn_awx_pa_t_kernel(tc, mid_logits, x, W2, b2, out):
         s_sq(0)
         g_sm(0, 0, 2)
         g_norm(0)
+        for a in range(4):
+            w_t(a)
+            w_ev(a, True)
+        w_q(0)
         relu(1)
         s_sq(1)
         g_sm(0, 2, 2)
         g_norm(1)
-        for ap in range(4):
-            w_t(ap)
-            if ap % 2 == 1:
-                w_q(ap // 2)
+        for a in range(4, 8):
+            w_t(a)
+            w_ev(a, True)
+        w_q(1)
         pe_th(0)
         pe_tx(0)
         evh(0)
@@ -421,11 +408,8 @@ def tile_bhcn_awx_pa_t_kernel(tc, mid_logits, x, W2, b2, out):
         evx(1)
         g_sm(1, 0, GT)
         g_norm(2)
-        pe_tx(2)
-        evx(2)
         relu(4)
         s_sq(4)
-        relu(5)
 
         for s in range(NPR):
             j0, j1 = 2 * s, 2 * s + 1
@@ -438,7 +422,7 @@ def tile_bhcn_awx_pa_t_kernel(tc, mid_logits, x, W2, b2, out):
             v_a(j0)
             newton_v()
             if ok(s + 5):
-                s_sq(s + 5)
+                relu(s + 5)
             newton_s()
             v_max(j0)
             if ok(s + 1):
@@ -448,23 +432,21 @@ def tile_bhcn_awx_pa_t_kernel(tc, mid_logits, x, W2, b2, out):
                 pe_mm(j0 + 2)
             if ok(s + 2):
                 pe_th(s + 2)
-            if ok(s + 3):
-                pe_tx(s + 3)
+                pe_tx(s + 2)
             exp_start(j0)
             g_fin(1)
             v_a(j1)
             newton_v()
             if ok(s + 1):
                 pe_mm(j1 + 2)
-            if ok(s + 3):
-                evx(s + 3)
+            if ok(s + 5):
+                s_sq(s + 5)
             newton_s()
             v_max(j1)
             if ok(s + 2):
                 evh(s + 2)
+                evx(s + 2)
             newton_s()
-            if ok(s + 6):
-                relu(s + 6)
             newton_v()
             g_fin(1)
         exp_start(NT - 1)

@@ -27,13 +27,13 @@ LN2 = math.log(2.0)
 ALPHA = LN2 / float(2 ** 23)
 BETA = LN2 * (0.043 - 127.0)
 
-PIN = True
+PIN = False
 NIT = 4
 BATCHES = [[4 * g, 4 * g + 1, 4 * g + 2, 4 * g + 3] for g in range(7)] + [[28, 29], [30], [31]]
-EVH_ON_V = (0, 1)
-EVX_ON_S = ()
-RELU_ON_S = tuple(range(16))
-FIN_ENG = {30: "V", 31: "V"}
+EVH_ON_V = ()
+EVX_ON_S = tuple(range(16))
+RELU_ON_S = ()
+FIN_ENG = dict((j, "S" if j % 4 == 1 else "V") for j in range(32))
 
 
 def tile_bhcn_awx_pa_t_kernel(tc, mid_logits, x, W2, b2, out):
@@ -79,6 +79,9 @@ def tile_bhcn_awx_pa_t_kernel(tc, mid_logits, x, W2, b2, out):
         make_identity(nc, ident_b[:])
         mhalf = keep.tile([P, GT], F32, name="mhalf")
         nc.gpsimd.memset(mhalf[:], -0.5)
+        kc = keep.tile([P, NIT], F32, name="kc")
+        for k in range(NIT):
+            nc.gpsimd.memset(kc[:, k : k + 1], float(k))
 
         wgrp = keep.tile([P, 2, L2, 4], BF16, name="wgrp", align_bytes=64)
         wc = keep.tile([P, 2, L2], U32, name="wc", align_bytes=64)
@@ -138,9 +141,9 @@ def tile_bhcn_awx_pa_t_kernel(tc, mid_logits, x, W2, b2, out):
             h = st["h", pr]
             hnp = work.tile([P, 2, 4, P], BF16, name="hnp")
             for jj in range(2):
-                nc.gpsimd.tensor_scalar(
-                    out=hnp[:, jj, :, :].rearrange("p (u e) q -> p u e q", u=2),
-                    in0=h[:, jj, :].rearrange("p (u q e) -> p u e q", u=2, e=2),
+                nc.vector.tensor_scalar(
+                    out=hnp[:, jj, :, :].rearrange("p t q -> p (t q)"),
+                    in0=h[:, jj, :],
                     scalar1=st["negmu", g][:, c0 + jj : c0 + jj + 1],
                     scalar2=st["rstd", g][:, c0 + jj : c0 + jj + 1],
                     op0=ALU.add,
@@ -199,22 +202,26 @@ def tile_bhcn_awx_pa_t_kernel(tc, mid_logits, x, W2, b2, out):
             else:
                 nc.vector.tensor_copy(out=xg, in_=src)
 
-        def w_t(a):
-            tw = psum.tile([P, 2, 2, P], F32, name="tw", tag="po", bufs=4)
-            ww = w_ch[a // 2][:, a % 2, :].bitcast(F32)
-            for g in range(2):
+        def w_t(ap):
+            twh = psum.tile([P, 2, 4, P], BF16, name="twh", tag="th")
+            twx = psum.tile([P, 2, 2, P], F32, name="twx", tag="tx")
+            for aa in range(2):
+                wrow = w_ch[ap][:, aa, :]
+                for t in range(4):
+                    nc.tensor.transpose(out=twh[:, aa, t, :], in_=wrow[:, P * t : P * (t + 1)], identity=ident_b[:])
+                ww = wrow.bitcast(F32)
                 for u in range(2):
-                    c0 = 256 * g + P * u
-                    nc.tensor.transpose(out=tw[:, g, u, :], in_=ww[:, c0 : c0 + P], identity=ident_f[:])
-            st["tw", a] = tw
-
-        def w_ev(a, on_v):
-            src = st["tw", a][:].rearrange("q g u n -> q g n u")
-            dst = wgrp[:].bitcast(F32)[:, :, a * P : (a + 1) * P, :]
-            if on_v:
-                nc.vector.tensor_copy(out=dst, in_=src)
-            else:
-                nc.scalar.copy(out=dst, in_=src)
+                    c0 = 256 + P * u
+                    nc.tensor.transpose(out=twx[:, aa, u, :], in_=ww[:, c0 : c0 + P], identity=ident_f[:])
+            rows = slice(2 * P * ap, 2 * P * (ap + 1))
+            nc.vector.tensor_copy(
+                out=wgrp[:, 0, rows, :].rearrange("p (a n) t -> p a n t", a=2),
+                in_=twh[:].rearrange("q a t n -> q a n t"),
+            )
+            nc.scalar.copy(
+                out=wgrp[:, 1, rows, :].bitcast(F32).rearrange("p (a n) u -> p a n u", a=2),
+                in_=twx[:].rearrange("q a u n -> q a n u"),
+            )
 
         def w_q(hf):
             cols = slice(hf * 512, (hf + 1) * 512)
@@ -267,8 +274,17 @@ def tile_bhcn_awx_pa_t_kernel(tc, mid_logits, x, W2, b2, out):
                 st["negM", bi] = small.tile([P, GT], F32, name="negM")
                 st["sume", bi] = small.tile([P, GT], F32, name="sume")
             li = st["li", j // 2]
-            nc.vector.tensor_reduce(
-                out=st["negM", bi][:, c : c + 1], in_=li[:, j % 2, :], axis=AX.X, op=ALU.max, negate=True
+            mx = work.tile([P, 512], BF16, name="mx", bufs=2)
+            mj = work.tile([P, 512], BF16, name="mj", bufs=2)
+            nc.vector.tensor_tensor(out=mx[:], in0=li[:, j % 2, 0:512], in1=li[:, j % 2, 512:1024], op=ALU.max)
+            nc.vector.tensor_scalar(
+                out=mj[:],
+                in0=mx[:],
+                scalar1=-1.0,
+                scalar2=None,
+                op0=ALU.mult,
+                op1=ALU.min,
+                accum_out=st["negM", bi][:, c : c + 1],
             )
 
         def s_exp(j):
@@ -285,32 +301,42 @@ def tile_bhcn_awx_pa_t_kernel(tc, mid_logits, x, W2, b2, out):
 
         def v_n0(bi):
             n = len(BATCHES[bi])
-            sc = small.tile([P, GT], F32, name="sc")
             y = small.tile([P, GT], F32, name="y0")
-            nc.vector.tensor_copy(out=sc[:, 0:n], in_=st["sume", bi][:, 0:n])
             nc.vector.tensor_scalar(
-                out=y[:, 0:n], in0=sc[:, 0:n].bitcast(I32), scalar1=ALPHA, scalar2=BETA, op0=ALU.mult, op1=ALU.add
+                out=y[:, 0:n],
+                in0=st["sume", bi][:, 0:n].bitcast(I32),
+                scalar1=ALPHA,
+                scalar2=BETA,
+                op0=ALU.mult,
+                op1=ALU.add,
             )
             st["y", bi] = y
+            st["it", bi] = 0
 
         def s_ne(bi):
             n = len(BATCHES[bi])
+            k = st["it", bi]
             e = small.tile([P, GT], F32, name="e")
-            nc.scalar.activation(out=e[:, 0:n], in_=st["y", bi][:, 0:n], func=ACT.Exp, scale=-1.0)
+            nc.scalar.activation(
+                out=e[:, 0:n], in_=st["y", bi][:, 0:n], func=ACT.Exp, scale=-1.0, bias=kc[:, k : k + 1]
+            )
             st["e", bi] = e
+            st["it", bi] = k + 1
 
         def v_nu(bi, last):
             n = len(BATCHES[bi])
             u = small.tile([P, GT], F32, name="u")
             y2 = small.tile([P, GT], F32, name="y2")
-            nc.vector.tensor_tensor(out=u[:, 0:n], in0=st["e", bi][:, 0:n], in1=st["sume", bi][:, 0:n], op=ALU.mult)
-            nc.vector.scalar_tensor_tensor(
-                out=y2[:, 0:n], in0=u[:, 0:n], scalar=-1.0, in1=st["y", bi][:, 0:n], op0=ALU.add, op1=ALU.add
-            )
+            nc.gpsimd.tensor_tensor(out=u[:, 0:n], in0=st["e", bi][:, 0:n], in1=st["sume", bi][:, 0:n], op=ALU.mult)
+            nc.gpsimd.tensor_tensor(out=y2[:, 0:n], in0=u[:, 0:n], in1=st["y", bi][:, 0:n], op=ALU.add)
             st["y", bi] = y2
             if last:
+                nm = small.tile([P, GT], F32, name="nm")
                 nsh = small.tile([P, GT], F32, name="nsh")
-                nc.vector.tensor_tensor(out=nsh[:, 0:n], in0=st["negM", bi][:, 0:n], in1=y2[:, 0:n], op=ALU.subtract)
+                nc.gpsimd.tensor_scalar(
+                    out=nm[:, 0:n], in0=st["negM", bi][:, 0:n], scalar1=float(NIT), scalar2=1.0, op0=ALU.add, op1=ALU.mult
+                )
+                nc.gpsimd.tensor_tensor(out=nsh[:, 0:n], in0=nm[:, 0:n], in1=y2[:, 0:n], op=ALU.subtract)
                 st["nsh", bi] = nsh
 
         def fin(j, eng):
@@ -325,6 +351,10 @@ def tile_bhcn_awx_pa_t_kernel(tc, mid_logits, x, W2, b2, out):
                     scalar2=1.0,
                     op0=ALU.add,
                     op1=ALU.mult,
+                )
+            elif eng == "S":
+                nc.scalar.activation(
+                    out=li[:, j % 2, :], in_=li[:, j % 2, :], func=ACT.Identity, bias=nsh[:, c : c + 1]
                 )
             else:
                 nc.vector.tensor_scalar(
@@ -380,18 +410,14 @@ def tile_bhcn_awx_pa_t_kernel(tc, mid_logits, x, W2, b2, out):
         s_sq(0)
         g_sm(0, 0, 2)
         g_norm(0)
-        for a in range(4):
-            w_t(a)
-            w_ev(a, True)
-        w_q(0)
         relu(1)
         s_sq(1)
         g_sm(0, 2, 2)
         g_norm(1)
-        for a in range(4, 8):
-            w_t(a)
-            w_ev(a, True)
-        w_q(1)
+        for ap in range(4):
+            w_t(ap)
+            if ap % 2 == 1:
+                w_q(ap // 2)
         pe_th(0)
         pe_tx(0)
         evh(0)
@@ -408,8 +434,11 @@ def tile_bhcn_awx_pa_t_kernel(tc, mid_logits, x, W2, b2, out):
         evx(1)
         g_sm(1, 0, GT)
         g_norm(2)
+        pe_tx(2)
+        evx(2)
         relu(4)
         s_sq(4)
+        relu(5)
 
         for s in range(NPR):
             j0, j1 = 2 * s, 2 * s + 1
@@ -422,7 +451,7 @@ def tile_bhcn_awx_pa_t_kernel(tc, mid_logits, x, W2, b2, out):
             v_a(j0)
             newton_v()
             if ok(s + 5):
-                relu(s + 5)
+                s_sq(s + 5)
             newton_s()
             v_max(j0)
             if ok(s + 1):
@@ -432,21 +461,23 @@ def tile_bhcn_awx_pa_t_kernel(tc, mid_logits, x, W2, b2, out):
                 pe_mm(j0 + 2)
             if ok(s + 2):
                 pe_th(s + 2)
-                pe_tx(s + 2)
+            if ok(s + 3):
+                pe_tx(s + 3)
             exp_start(j0)
             g_fin(1)
             v_a(j1)
             newton_v()
             if ok(s + 1):
                 pe_mm(j1 + 2)
-            if ok(s + 5):
-                s_sq(s + 5)
+            if ok(s + 3):
+                evx(s + 3)
             newton_s()
             v_max(j1)
             if ok(s + 2):
                 evh(s + 2)
-                evx(s + 2)
             newton_s()
+            if ok(s + 6):
+                relu(s + 6)
             newton_v()
             g_fin(1)
         exp_start(NT - 1)

@@ -29,11 +29,11 @@ BETA = LN2 * (0.043 - 127.0)
 
 PIN = False
 NIT = 4
-BATCHES = [[4 * g, 4 * g + 1, 4 * g + 2, 4 * g + 3] for g in range(7)] + [[28, 29], [30], [31]]
+BATCHES = [[4 * g, 4 * g + 1, 4 * g + 2, 4 * g + 3] for g in range(8)]
 EVH_ON_V = ()
 EVX_ON_S = tuple(range(16))
 RELU_ON_S = ()
-FIN_ENG = dict((j, "S" if j % 4 == 1 else "V") for j in range(32))
+FIN_ENG = dict((j, "S" if (j % 4 == 1 or j == 31) else "V") for j in range(32))
 
 
 def tile_bhcn_awx_pa_t_kernel(tc, mid_logits, x, W2, b2, out):
@@ -393,15 +393,23 @@ def tile_bhcn_awx_pa_t_kernel(tc, mid_logits, x, W2, b2, out):
         def exp_start(j):
             s_exp(j)
             for bi, bt in enumerate(BATCHES):
-                if bt[-1] == j:
+                if bt[-1] == j and bi < len(BATCHES) - 1:
                     pending.append([bi, 0])
+            if j == NT - 1:
+                bi = len(BATCHES) - 1
+                lns = small.tile([P, GT], F32, name="lns")
+                nsh = small.tile([P, GT], F32, name="nsh")
+                nc.scalar.activation(out=lns[:], in_=st["sume", bi][:], func=ACT.Ln)
+                nc.vector.tensor_tensor(out=nsh[:], in0=st["negM", bi][:], in1=lns[:], op=ALU.subtract)
+                st["nsh", bi] = nsh
+                st["last_ready"] = True
 
         def g_fin(k):
             for i in range(k):
                 if fin_q:
                     j = fin_q.pop(0)
                     fin(j, FIN_ENG.get(j, "G"))
-                    if j >= NT - 2:
+                    if j >= NT - 4:
                         store(j, 1)
                     elif j % 2 == 1:
                         store(j - 1, 2)
@@ -485,3 +493,5 @@ def tile_bhcn_awx_pa_t_kernel(tc, mid_logits, x, W2, b2, out):
             newton_v()
             newton_s()
             g_fin(4)
+        fin_q.extend(BATCHES[-1])
+        g_fin(4)

@@ -29,6 +29,7 @@ BETA = LN2 * (0.043 - 127.0)
 
 PIN = False
 NIT = 4
+LN_STEP = 1.0 / 128.0
 BATCHES = [[4 * g, 4 * g + 1, 4 * g + 2, 4 * g + 3] for g in range(8)]
 EVH_ON_V = ()
 EVX_ON_S = tuple(range(16))
@@ -79,6 +80,10 @@ def tile_bhcn_awx_pa_t_kernel(tc, mid_logits, x, W2, b2, out):
         make_identity(nc, ident_b[:])
         mhalf = keep.tile([P, GT], F32, name="mhalf")
         nc.gpsimd.memset(mhalf[:], -0.5)
+        peps = keep.tile([P, GT], F32, name="peps")
+        meps = keep.tile([P, GT], F32, name="meps")
+        nc.gpsimd.memset(peps[:], LN_STEP)
+        nc.gpsimd.memset(meps[:], -LN_STEP)
         kc = keep.tile([P, NIT], F32, name="kc")
         for k in range(NIT):
             nc.gpsimd.memset(kc[:, k : k + 1], float(k))
@@ -339,6 +344,29 @@ def tile_bhcn_awx_pa_t_kernel(tc, mid_logits, x, W2, b2, out):
                 nc.gpsimd.tensor_tensor(out=nsh[:, 0:n], in0=nm[:, 0:n], in1=y2[:, 0:n], op=ALU.subtract)
                 st["nsh", bi] = nsh
 
+        def g_ln(bi):
+            s = st["sume", bi][:]
+            t = [small.tile([P, GT], F32, name="gl%d" % i) for i in range(10)]
+            nsh = small.tile([P, GT], F32, name="nsh")
+            nc.gpsimd.tensor_tensor(out=t[0][:], in0=s, in1=peps[:], op=ALU.pow)
+            nc.gpsimd.tensor_tensor(out=t[1][:], in0=s, in1=meps[:], op=ALU.pow)
+            nc.gpsimd.tensor_tensor(out=t[2][:], in0=t[0][:], in1=t[1][:], op=ALU.subtract)
+            nc.gpsimd.tensor_tensor(out=t[3][:], in0=t[2][:], in1=t[2][:], op=ALU.mult)
+            nc.gpsimd.tensor_scalar(
+                out=t[4][:], in0=t[3][:], scalar1=-15.0 / 21504.0, scalar2=3.0 / 640.0, op0=ALU.mult, op1=ALU.add
+            )
+            nc.gpsimd.tensor_tensor(out=t[5][:], in0=t[4][:], in1=t[3][:], op=ALU.mult)
+            nc.gpsimd.tensor_scalar(
+                out=t[6][:], in0=t[5][:], scalar1=-1.0 / 24.0, scalar2=1.0, op0=ALU.add, op1=ALU.mult
+            )
+            nc.gpsimd.tensor_tensor(out=t[7][:], in0=t[6][:], in1=t[3][:], op=ALU.mult)
+            nc.gpsimd.tensor_scalar(
+                out=t[8][:], in0=t[7][:], scalar1=1.0, scalar2=-0.5 / LN_STEP, op0=ALU.add, op1=ALU.mult
+            )
+            nc.gpsimd.tensor_tensor(out=t[9][:], in0=t[8][:], in1=t[2][:], op=ALU.mult)
+            nc.gpsimd.tensor_tensor(out=nsh[:], in0=t[9][:], in1=st["negM", bi][:], op=ALU.add)
+            st["nsh", bi] = nsh
+
         def fin(j, eng):
             bi, c = bt_of(j)
             li = st["li", j // 2]
@@ -394,7 +422,8 @@ def tile_bhcn_awx_pa_t_kernel(tc, mid_logits, x, W2, b2, out):
             s_exp(j)
             for bi, bt in enumerate(BATCHES):
                 if bt[-1] == j and bi < len(BATCHES) - 1:
-                    pending.append([bi, 0])
+                    g_ln(bi)
+                    fin_q.extend(bt)
             if j == NT - 1:
                 bi = len(BATCHES) - 1
                 lns = small.tile([P, GT], F32, name="lns")

import math
from contextlib import ExitStack

import concourse.mybir as mybir
from concourse.masks import make_identity

F32 = mybir.dt.float32
BF16 = mybir.dt.bfloat16
U32 = mybir.dt.uint32
U8 = mybir.dt.uint8
I32 = mybir.dt.int32
FP8X4 = mybir.dt.float8_e4m3fn_x4
ALU = mybir.AluOpType
ACT = mybir.ActivationFunctionType
AX = mybir.AxisListType

P = 128
B, D, L1, L2 = 4096, 512, 512, 1024
NT = B // P
NPR = NT // 2
GT = 4
NG = NT // GT
LN_EPS = 1e-5
FLOPS = 2 * B * (L1 + D) * L2

LN2 = math.log(2.0)
ALPHA = LN2 / float(2 ** 23)
BETA = LN2 * (0.043 - 127.0)

PIN = False
NIT = 4
LN_STEP = 1.0 / 128.0
BATCHES = [[4 * g, 4 * g + 1, 4 * g + 2, 4 * g + 3] for g in range(8)]
EVH_ON_V = ()
EVX_ON_S = tuple(range(16))
RELU_ON_S = ()
FIN_ENG = dict((j, "S" if (j % 4 == 1 or j == 31) else "V") for j in range(32))


def tile_bhcn_awx_pa_t_kernel(tc, mid_logits, x, W2, b2, out):
    nc = tc.nc
    m_v = mid_logits.rearrange("(p j) k -> p j k", j=NT)
    x_v = x.rearrange("(p j) k -> p j k", j=NT)
    o_v = out.rearrange("(p j) n -> p j n", j=NT)
    w_v = W2.rearrange("(a p) k -> p a k", p=P)

    with ExitStack() as ctx:
        if PIN:
            ctx.enter_context(tc.manual_schedule())
        keep = ctx.enter_context(tc.tile_pool(name="keep", bufs=1))
        work = ctx.enter_context(tc.tile_pool(name="work", bufs=4))
        small = ctx.enter_context(tc.tile_pool(name="small", bufs=5))
        lip = ctx.enter_context(tc.tile_pool(name="lip", bufs=7))
        psum = ctx.enter_context(tc.psum_pool(name="psum", bufs=2))

        m_ch = []
        x_ch = []
        w_ch = []
        for g in range(NG):
            m_ch.append(keep.tile([P, GT, L1], BF16, name="m%d" % g))
            x_ch.append(keep.tile([P, GT, D], BF16, name="x%d" % g))
        for c in range(4):
            w_ch.append(keep.tile([P, 2, L1 + D], BF16, name="w%d" % c))
        b_bc = keep.tile([P, L2], BF16, name="b_bc")

        nc.sync.dma_start(out=m_ch[0][:], in_=m_v[:, 0:GT, :])
        for c in range(4):
            nc.sync.dma_start(out=w_ch[c][:], in_=w_v[:, 2 * c : 2 * c + 2, :])
        nc.sync.dma_start(out=x_ch[0][:], in_=x_v[:, 0:GT, :])
        nc.sync.dma_start(out=m_ch[1][:], in_=m_v[:, GT : 2 * GT, :])
        nc.sync.dma_start(out=b_bc[:], in_=b2.partition_broadcast(P))
        nc.sync.dma_start(out=x_ch[1][:], in_=x_v[:, GT : 2 * GT, :])
        for g in range(2, NG):
            nc.sync.dma_start(out=m_ch[g][:], in_=m_v[:, GT * g : GT * (g + 1), :])
            nc.sync.dma_start(out=x_ch[g][:], in_=x_v[:, GT * g : GT * (g + 1), :])

        ident_f = keep.tile([P, P], F32, name="ident_f")
        ident_b = keep.tile([P, P], BF16, name="ident_b")
        make_identity(nc, ident_f[:])
        make_identity(nc, ident_b[:])
        mhalf = keep.tile([P, GT], F32, name="mhalf")
        nc.gpsimd.memset(mhalf[:], -0.5)
        peps = keep.tile([P, GT], F32, name="peps")
        meps = keep.tile([P, GT], F32, name="meps")
        nc.gpsimd.memset(peps[:], LN_STEP)
        nc.gpsimd.memset(meps[:], -LN_STEP)
        kc = keep.tile([P, NIT], F32, name="kc")
        for k in range(NIT):
            nc.gpsimd.memset(kc[:, k : k + 1], float(k))

        wgrp = keep.tile([P, 2, L2, 4], BF16, name="wgrp", align_bytes=64)
        wc = keep.tile([P, 2, L2], U32, name="wc", align_bytes=64)
        ws = keep.tile([P, 2, L2], U8, name="ws", align_bytes=64)

        st = {}

        def relu(pr):
            g, c0 = pr // 2, 2 * (pr % 2)
            if c0 == 0:
                for nm in ("sum_h", "negmu", "ssq", "var", "rstd"):
                    st[nm, g] = small.tile([P, GT], F32, name=nm)
            h = work.tile([P, 2, L1], BF16, name="h", bufs=6)
            for jj in range(2):
                j = 2 * pr + jj
                acc = st["sum_h", g][:, c0 + jj : c0 + jj + 1]
                if pr in RELU_ON_S:
                    nc.scalar.activation(
                        out=h[:, jj, :], in_=m_ch[j // GT][:, j % GT, :], func=ACT.Relu, accum_out=acc
                    )
                else:
                    nc.vector.tensor_scalar(
                        out=h[:, jj, :],
                        in0=m_ch[j // GT][:, j % GT, :],
                        scalar1=0.0,
                        scalar2=None,
                        op0=ALU.max,
                        op1=ALU.add,
                        accum_out=acc,
                    )
            st["h", pr] = h

        def s_sq(pr):
            g, c0 = pr // 2, 2 * (pr % 2)
            h = st["h", pr]
            nc.scalar.mul(out=st["negmu", g][:, c0 : c0 + 2], in_=st["sum_h", g][:, c0 : c0 + 2], mul=-1.0 / L1)
            for jj in range(2):
                sqj = work.tile([P, L1], BF16, name="sqj", bufs=2)
                nc.scalar.activation(
                    out=sqj[:],
                    in_=h[:, jj, :],
                    func=ACT.Square,
                    bias=st["negmu", g][:, c0 + jj : c0 + jj + 1],
                    accum_out=st["ssq", g][:, c0 + jj : c0 + jj + 1],
                )

        def g_sm(g, c0, n):
            cs = slice(c0, c0 + n)
            var, rstd = (st[nm, g][:, cs] for nm in ("var", "rstd"))
            nc.gpsimd.tensor_scalar(
                out=var, in0=st["ssq", g][:, cs], scalar1=1.0 / L1, scalar2=LN_EPS, op0=ALU.mult, op1=ALU.add
            )
            nc.gpsimd.tensor_tensor(out=rstd, in0=var, in1=mhalf[:, 0:n], op=ALU.pow)

        def g_norm(pr):
            g, c0 = pr // 2, 2 * (pr % 2)
            h = st["h", pr]
            hnp = work.tile([P, 2, 4, P], BF16, name="hnp")
            for jj in range(2):
                nc.vector.tensor_scalar(
                    out=hnp[:, jj, :, :].rearrange("p t q -> p (t q)"),
                    in0=h[:, jj, :],
                    scalar1=st["negmu", g][:, c0 + jj : c0 + jj + 1],
                    scalar2=st["rstd", g][:, c0 + jj : c0 + jj + 1],
                    op0=ALU.add,
                    op1=ALU.mult,
                )
            st["hnp", pr] = hnp

        def pe_th(pr):
            hnp = st["hnp", pr]
            th = psum.tile([P, 2, 4, P], BF16, name="th")
            for jj in range(2):
                for t in range(4):
                    nc.tensor.transpose(out=th[:, jj, t, :], in_=hnp[:, jj, t, :], identity=ident_b[:])
            st["th", pr] = th

        def evh(pr):
            th = st["th", pr]
            hg = grouped(pr)[:, 0, :, :, :]
            src = th[:].rearrange("q j t b -> q j b t")
            if pr in EVH_ON_V:
                nc.vector.tensor_copy(out=hg, in_=src)
            else:
                nc.scalar.copy(out=hg, in_=src)

        def grouped(pr):
            if ("cg", pr) not in st:
                st["cg", pr] = work.tile([P, 2, 2, P, 4], BF16, name="cg", align_bytes=64)
            return st["cg", pr]

        def v_q(pr):
            cg = st["cg", pr]
            cc = work.tile([P, 4 * P], U32, name="cc", align_bytes=64)
            cs = work.tile([P, 4 * P], U8, name="cs", align_bytes=64)
            nc.vector.quantize_mx(
                out=cc[:].bitcast(FP8X4), scales=cs[:], in_=cg[:].rearrange("p g j b t -> p (g j b t)")
            )
            st["cq", pr] = (cc, cs)

        def pe_tx(pr):
            tx = psum.tile([P, 2, 2, P], F32, name="tx")
            for jj in range(2):
                j = 2 * pr + jj
                xw = x_ch[j // GT][:, j % GT, :].bitcast(F32)
                for u in range(2):
                    nc.tensor.transpose(
                        out=tx[:, jj, u, :], in_=xw[:, P * u : P * (u + 1)], identity=ident_f[:]
                    )
            st["tx", pr] = tx

        def evx(pr):
            tx = st["tx", pr]
            xg = grouped(pr)[:, 1, :, :, :].bitcast(F32)
            src = tx[:].rearrange("q j u b -> q j b u")
            if pr in EVX_ON_S:
                nc.scalar.copy(out=xg, in_=src)
            else:
                nc.vector.tensor_copy(out=xg, in_=src)

        def w_t(ap):
            twh = psum.tile([P, 2, 4, P], BF16, name="twh", tag="th")
            twx = psum.tile([P, 2, 2, P], F32, name="twx", tag="tx")
            for aa in range(2):
                wrow = w_ch[ap][:, aa, :]
                for t in range(4):
                    nc.tensor.transpose(out=twh[:, aa, t, :], in_=wrow[:, P * t : P * (t + 1)], identity=ident_b[:])
                ww = wrow.bitcast(F32)
                for u in range(2):
                    c0 = 256 + P * u
                    nc.tensor.transpose(out=twx[:, aa, u, :], in_=ww[:, c0 : c0 + P], identity=ident_f[:])
            rows = slice(2 * P * ap, 2 * P * (ap + 1))
            nc.vector.tensor_copy(
                out=wgrp[:, 0, rows, :].rearrange("p (a n) t -> p a n t", a=2),
                in_=twh[:].rearrange("q a t n -> q a n t"),
            )
            nc.scalar.copy(
                out=wgrp[:, 1, rows, :].bitcast(F32).rearrange("p (a n) u -> p a n u", a=2),
                in_=twx[:].rearrange("q a u n -> q a n u"),
            )

        def w_q(hf):
            cols = slice(hf * 512, (hf + 1) * 512)
            for g in range(2):
                nc.vector.quantize_mx(
                    out=wc[:, g, cols].bitcast(FP8X4),
                    scales=ws[:, g, cols],
                    in_=wgrp[:, g, cols, :].rearrange("p n t -> p (n t)"),
                )

        def pe_mm(j):
            pr, jj = j // 2, j % 2
            cc, ss = st["cq", pr]
            pos = []
            for hf in range(2):
                pos.append(psum.tile([P, 512], F32, name="po", tag="po", bufs=4))
            for g in range(2):
                bcols = slice((2 * g + jj) * P, (2 * g + jj + 1) * P)
                for hf in range(2):
                    cols = slice(hf * 512, (hf + 1) * 512)
                    nc.tensor.matmul_mx(
                        out=pos[hf][:],
                        lhsT=cc[:, bcols].bitcast(FP8X4),
                        lhsT_scale=ss[:, bcols],
                        rhs=wc[:, g, cols].bitcast(FP8X4),
                        rhs_scale=ws[:, g, cols],
                        start=(g == 0),
                        stop=(g == 1),
                    )
            st["po", j] = pos

        def v_a(j):
            if j % 2 == 0:
                st["li", j // 2] = lip.tile([P, 2, L2], F32, name="li")
            li = st["li", j // 2]
            pos = st["po", j]
            for hf in range(2):
                cols = slice(hf * 512, (hf + 1) * 512)
                nc.vector.tensor_tensor(out=li[:, j % 2, cols], in0=pos[hf][:], in1=b_bc[:, cols], op=ALU.add)

        def bt_of(j):
            for bi, bt in enumerate(BATCHES):
                if j in bt:
                    return bi, bt.index(j)
            return None

        def v_max(j):
            bi, c = bt_of(j)
            if c == 0:
                st["negM", bi] = small.tile([P, GT], F32, name="negM")
                st["sume", bi] = small.tile([P, GT], F32, name="sume")
            li = st["li", j // 2]
            mx = work.tile([P, 512], BF16, name="mx", bufs=2)
            mj = work.tile([P, 512], BF16, name="mj", bufs=2)
            nc.vector.tensor_tensor(out=mx[:], in0=li[:, j % 2, 0:512], in1=li[:, j % 2, 512:1024], op=ALU.max)
            nc.vector.tensor_scalar(
                out=mj[:],
                in0=mx[:],
                scalar1=-1.0,
                scalar2=None,
                op0=ALU.mult,
                op1=ALU.min,
                accum_out=st["negM", bi][:, c : c + 1],
            )

        def s_exp(j):
            bi, c = bt_of(j)
            li = st["li", j // 2]
            ej = work.tile([P, L2], BF16, name="ej", bufs=2)
            nc.scalar.activation(
                out=ej[:],
                in_=li[:, j % 2, :],
                func=ACT.Exp,
                bias=st["negM", bi][:, c : c + 1],
                accum_out=st["sume", bi][:, c : c + 1],
            )

        def v_n0(bi):
            n = len(BATCHES[bi])
            y = small.tile([P, GT], F32, name="y0")
            nc.vector.tensor_scalar(
                out=y[:, 0:n],
                in0=st["sume", bi][:, 0:n].bitcast(I32),
                scalar1=ALPHA,
                scalar2=BETA,
                op0=ALU.mult,
                op1=ALU.add,
            )
            st["y", bi] = y
            st["it", bi] = 0

        def s_ne(bi):
            n = len(BATCHES[bi])
            k = st["it", bi]
            e = small.tile([P, GT], F32, name="e")
            nc.scalar.activation(
                out=e[:, 0:n], in_=st["y", bi][:, 0:n], func=ACT.Exp, scale=-1.0, bias=kc[:, k : k + 1]
            )
            st["e", bi] = e
            st["it", bi] = k + 1

        def v_nu(bi, last):
            n = len(BATCHES[bi])
            u = small.tile([P, GT], F32, name="u")
            y2 = small.tile([P, GT], F32, name="y2")
            nc.gpsimd.tensor_tensor(out=u[:, 0:n], in0=st["e", bi][:, 0:n], in1=st["sume", bi][:, 0:n], op=ALU.mult)
            nc.gpsimd.tensor_tensor(out=y2[:, 0:n], in0=u[:, 0:n], in1=st["y", bi][:, 0:n], op=ALU.add)
            st["y", bi] = y2
            if last:
                nm = small.tile([P, GT], F32, name="nm")
                nsh = small.tile([P, GT], F32, name="nsh")
                nc.gpsimd.tensor_scalar(
                    out=nm[:, 0:n], in0=st["negM", bi][:, 0:n], scalar1=float(NIT), scalar2=1.0, op0=ALU.add, op1=ALU.mult
                )
                nc.gpsimd.tensor_tensor(out=nsh[:, 0:n], in0=nm[:, 0:n], in1=y2[:, 0:n], op=ALU.subtract)
                st["nsh", bi] = nsh

        def g_ln(bi):
            s = st["sume", bi][:]
            t = [small.tile([P, GT], F32, name="gl%d" % i) for i in range(10)]
            nsh = small.tile([P, GT], F32, name="nsh")
            nc.gpsimd.tensor_tensor(out=t[0][:], in0=s, in1=peps[:], op=ALU.pow)
            nc.gpsimd.tensor_tensor(out=t[1][:], in0=s, in1=meps[:], op=ALU.pow)
            nc.gpsimd.tensor_tensor(out=t[2][:], in0=t[0][:], in1=t[1][:], op=ALU.subtract)
            nc.gpsimd.tensor_tensor(out=t[3][:], in0=t[2][:], in1=t[2][:], op=ALU.mult)
            nc.gpsimd.tensor_scalar(
                out=t[4][:], in0=t[3][:], scalar1=-15.0 / 21504.0, scalar2=3.0 / 640.0, op0=ALU.mult, op1=ALU.add
            )
            nc.gpsimd.tensor_tensor(out=t[5][:], in0=t[4][:], in1=t[3][:], op=ALU.mult)
            nc.gpsimd.tensor_scalar(
                out=t[6][:], in0=t[5][:], scalar1=-1.0 / 24.0, scalar2=1.0, op0=ALU.add, op1=ALU.mult
            )
            nc.gpsimd.tensor_tensor(out=t[7][:], in0=t[6][:], in1=t[3][:], op=ALU.mult)
            nc.gpsimd.tensor_scalar(
                out=t[8][:], in0=t[7][:], scalar1=1.0, scalar2=-0.5 / LN_STEP, op0=ALU.add, op1=ALU.mult
            )
            nc.gpsimd.tensor_tensor(out=t[9][:], in0=t[8][:], in1=t[2][:], op=ALU.mult)
            nc.gpsimd.tensor_tensor(out=nsh[:], in0=t[9][:], in1=st["negM", bi][:], op=ALU.add)
            st["nsh", bi] = nsh

        def fin(j, eng):
            bi, c = bt_of(j)
            li = st["li", j // 2]
            nsh = st["nsh", bi]
            if eng == "G":
                nc.gpsimd.tensor_scalar(
                    out=li[:, j % 2, :],
                    in0=li[:, j % 2, :],
                    scalar1=nsh[:, c : c + 1],
                    scalar2=1.0,
                    op0=ALU.add,
                    op1=ALU.mult,
                )
            elif eng == "S":
                nc.scalar.activation(
                    out=li[:, j % 2, :], in_=li[:, j % 2, :], func=ACT.Identity, bias=nsh[:, c : c + 1]
                )
            else:
                nc.vector.tensor_scalar(
                    out=li[:, j % 2, :], in0=li[:, j % 2, :], scalar1=nsh[:, c : c + 1], scalar2=None, op0=ALU.add
                )

        def store(j0, n):
            li = st["li", j0 // 2]
            nc.sync.dma_start(out=o_v[:, j0 : j0 + n, :], in_=li[:, j0 % 2 : j0 % 2 + n, :])

        def ok(pr):
            return 0 <= pr < NPR

        pending = []
        fin_q = []

        def newton_v():
            for item in pending:
                if item[1] % 2 == 0 and item[1] <= 2 * NIT:
                    if item[1] == 0:
                        v_n0(item[0])
                    else:
                        v_nu(item[0], item[1] == 2 * NIT)
                    item[1] += 1
                    break
            while pending and pending[0][1] == 2 * NIT + 1:
                fin_q.extend(BATCHES[pending.pop(0)[0]])

        def newton_s():
            for item in pending:
                if item[1] % 2 == 1:
                    s_ne(item[0])
                    item[1] += 1
                    break

        def exp_start(j):
            s_exp(j)
            for bi, bt in enumerate(BATCHES):
                if bt[-1] == j and bi < len(BATCHES) - 1:
                    g_ln(bi)
                    fin_q.extend(bt)
            if j == NT - 1:
                bi = len(BATCHES) - 1
                lns = small.tile([P, GT], F32, name="lns")
                nsh = small.tile([P, GT], F32, name="nsh")
                nc.scalar.activation(out=lns[:], in_=st["sume", bi][:], func=ACT.Ln)
                nc.vector.tensor_tensor(out=nsh[:], in0=st["negM", bi][:], in1=lns[:], op=ALU.subtract)
                st["nsh", bi] = nsh
                st["last_ready"] = True

        def g_fin(k):
            for i in range(k):
                if fin_q:
                    j = fin_q.pop(0)
                    fin(j, FIN_ENG.get(j, "G"))
                    if j >= NT - 4:
                        store(j, 1)
                    elif j % 2 == 1:
                        store(j - 1, 2)

        relu(0)
        s_sq(0)
        g_sm(0, 0, 2)
        g_norm(0)
        relu(1)
        s_sq(1)
        g_sm(0, 2, 2)
        g_norm(1)
        for ap in range(4):
            w_t(ap)
            if ap % 2 == 1:
                w_q(ap // 2)
        pe_th(0)
        pe_tx(0)
        evh(0)
        evx(0)
        v_q(0)
        pe_mm(0)
        pe_mm(1)
        pe_th(1)
        pe_tx(1)
        for pr in (2, 3):
            relu(pr)
            s_sq(pr)
        evh(1)
        evx(1)
        g_sm(1, 0, GT)
        g_norm(2)
        pe_tx(2)
        evx(2)
        relu(4)
        s_sq(4)
        relu(5)

        for s in range(NPR):
            j0, j1 = 2 * s, 2 * s + 1
            if s % 2 == 1 and ok(s + 3):
                g_sm((s + 3) // 2, 0, GT)
            if ok(s + 3):
                g_norm(s + 3)
            if s > 0:
                exp_start(j0 - 1)
            v_a(j0)
            newton_v()
            if ok(s + 5):
                s_sq(s + 5)
            newton_s()
            v_max(j0)
            if ok(s + 1):
                v_q(s + 1)
            newton_v()
            if ok(s + 1):
                pe_mm(j0 + 2)
            if ok(s + 2):
                pe_th(s + 2)
            if ok(s + 3):
                pe_tx(s + 3)
            exp_start(j0)
            g_fin(1)
            v_a(j1)
            newton_v()
            if ok(s + 1):
                pe_mm(j1 + 2)
            if ok(s + 3):
                evx(s + 3)
            newton_s()
            v_max(j1)
            if ok(s + 2):
                evh(s + 2)
            newton_s()
            if ok(s + 6):
                relu(s + 6)
            newton_v()
            g_fin(1)
        exp_start(NT - 1)
        while pending or fin_q:
            newton_v()
            newton_s()
            g_fin(4)
        fin_q.extend(BATCHES[-1])
        g_fin(4)
